import numpy as np
import ml_dtypes


def mxq(x, axis, fmt="e4m3"):
    dtype, down = {"e4m3": (ml_dtypes.float8_e4m3fn, 7), "e5m2": (ml_dtypes.float8_e5m2, 14)}[fmt]
    v = np.moveaxis(np.asarray(x, np.float32).astype(ml_dtypes.bfloat16).astype(np.float64), axis, -1)
    blocks = v.reshape(v.shape[:-1] + (-1, 32))
    amax = np.abs(blocks).max(-1, keepdims=True)
    byte = np.maximum(np.where(amax > 0, np.frexp(amax)[1] - 1 + 127, 0) - down, 1)
    scale = np.exp2(byte - 127.0)
    codes = (blocks / scale).astype(np.float32).astype(dtype).astype(np.float64)
    return np.moveaxis((codes * scale).reshape(v.shape), -1, axis)


WIDE = False


def mx_kscale(k):
    if not WIDE:
        return np.ones(k)
    levels = np.array([10, -10, 5, -5, 0])
    if k % 512:
        return np.exp2(np.random.permutation(np.resize(levels, k // 32))).repeat(32)
    a = np.empty((k // 512, 16))
    for p in range(k // 512):
        a[p, :8] = np.random.permutation(np.resize(levels, 8))
        for g in range(8):
            far = levels[np.abs(levels - a[p, g]) >= 10]
            a[p, g + 8] = far[np.random.randint(len(far))]
    return np.exp2(a.ravel()).repeat(32)


BF16 = ml_dtypes.bfloat16


def bf(x):
    return np.asarray(x, np.float32).astype(BF16)


def f64(x):
    return np.asarray(x).astype(np.float64)


B, C, NH, GW, GH, GZ = 2, 2048, 2, 16, 16, 16
N = GW * GH * GZ
D = C // NH
XS = 2.0


def setup_inputs():
    s, t = mx_kscale(C), mx_kscale(D)
    g = np.random.standard_normal((B, NH, D, D)) * np.sqrt(1.0 + C / N)
    e = np.exp(g - g.max(-1, keepdims=True))
    attn = e / e.sum(-1, keepdims=True)
    return {"x": bf(XS * np.random.standard_normal((B, C, GW, GH, GZ)) * s[None, :, None, None, None]),
            "w_v": bf(np.random.standard_normal((C, C)) / np.sqrt(C) / s[:, None] * np.tile(t, NH)[None, :]),
            "attn": bf(attn / t)}


def reference(x, w_v, attn):
    xt = f64(x).reshape(B, C, N).transpose(0, 2, 1)
    v = mxq(xt, 2, "e4m3") @ mxq(f64(w_v), 0, "e4m3")
    v = v.reshape(B, N, NH, D).transpose(0, 2, 3, 1)
    out = mxq(f64(attn), 3, "e4m3") @ mxq(v, 2, "e4m3")
    out = out.transpose(0, 3, 1, 2).reshape(B, N, C)
    return out.reshape(B, GW, GH, GZ, C).transpose(0, 4, 1, 2, 3)

@@ -1,0 +1,307 @@
+from contextlib import ExitStack
+
+import concourse.mybir as mybir
+from concourse.masks import make_identity
+
+B, C, NTOK, NH = 2, 2048, 4096, 2
+D = C // NH
+FLOPS = 2 * B * NTOK * C * C + 2 * B * NH * D * D * NTOK
+
+F32 = mybir.dt.float32
+BF16 = mybir.dt.bfloat16
+U32 = mybir.dt.uint32
+U8 = mybir.dt.uint8
+FP8X4 = mybir.dt.float8_e4m3fn_x4
+
+P = 128
+PACK = 4
+KP = P * PACK
+CH = 512
+NCH = B * NTOK // CH
+CPB = NTOK // CH
+G1 = C // KP
+G2 = D // KP
+NOB = C // KP
+NS1 = NCH * NOB
+LAG = 4
+NIT = D // P
+RAW_BUFS = 10
+NRUN = 16
+
+
+def s1_unit(k):
+    if k < 2 * NOB:
+        return (k % 2, k // 2)
+    return (k // NOB, k % NOB)
+
+
+def s2_unit(j):
+    if j < 2 * NOB:
+        return ((j // 2) % 2, j // 4, j % 2)
+    return (j // 4, (j // 2) % 2, j % 2)
+
+
+def run_step(r):
+    if r < 8:
+        return r
+    return 12 + 2 * (r - 8)
+
+
+def fresh_plan(k):
+    if k == 0:
+        return [([(("x", 0, g), True), (("w", g, 0), False)], [("x", 0, g), ("w", g, 0)], g) for g in range(G1)]
+    if k == 1:
+        piece = [("x", 1, g) for g in range(G1)]
+    elif k == 2:
+        piece = [("w", g, 1) for g in range(G1)]
+    else:
+        return []
+    return [([(piece[0], False)], [piece[0]], 0),
+            ([(piece[2], True), (piece[1], False)], [piece[1]], 1),
+            ([(piece[3], False)], [piece[2]], 2),
+            ([], [piece[3]], 3)]
+
+
+def ahead_jobs(k):
+    jobs = []
+    if 2 <= k < 6:
+        ob = k // 2 + 1
+        g0 = 2 * (k % 2)
+        jobs.append((("w", g0, ob), False))
+        jobs.append((("w", g0 + 1, ob), True))
+    if k >= 4 and k // 4 + 1 < NCH:
+        jobs.append((("x", k // 4 + 1, k % 4), False))
+    return jobs
+
+
+def tile_channelattention_pb_l_kernel(tc, x, w_v, attn, out):
+    nc = tc.nc
+    xv = x.rearrange("b c w h z -> b c (w h z)")
+    ov = out.rearrange("b c w h z -> b c (w h z)")
+
+    order = []
+    for k in range(NS1):
+        for ints, quants, g in fresh_plan(k):
+            for job, on_scalar in ints:
+                order.append(job)
+        for job, on_scalar in ahead_jobs(k):
+            order.append(job)
+
+    with ExitStack() as ctx:
+        const = ctx.enter_context(tc.tile_pool(name="const", bufs=1))
+        keep = ctx.enter_context(tc.tile_pool(name="keep", bufs=1))
+        raw = ctx.enter_context(tc.tile_pool(name="raw", bufs=RAW_BUFS))
+        araw = ctx.enter_context(tc.tile_pool(name="araw", bufs=3))
+        grp = ctx.enter_context(tc.tile_pool(name="grp", bufs=4))
+        agrp = ctx.enter_context(tc.tile_pool(name="agrp", bufs=4))
+        xq = ctx.enter_context(tc.tile_pool(name="xq", bufs=3))
+        vbp = ctx.enter_context(tc.tile_pool(name="vbp", bufs=3))
+        vq = ctx.enter_context(tc.tile_pool(name="vq", bufs=4))
+        outp = ctx.enter_context(tc.tile_pool(name="outp", bufs=3))
+        psum = ctx.enter_context(tc.psum_pool(name="psum", bufs=8))
+        ctx.enter_context(tc.manual_schedule())
+
+        warm_in = const.tile([P, 8], F32, name="warm_in", tag="warm_in")
+        warm_out = const.tile([P, 8], F32, name="warm_out", tag="warm_out")
+        nc.vector.memset(warm_in[:], 0.0)
+        nc.scalar.copy(out=warm_out[:], in_=warm_in[:])
+        ident = const.tile([P, P], F32, name="ident", tag="ident")
+        make_identity(nc, ident[:])
+
+        wc = []
+        ws = []
+        for ob in range(NOB):
+            wc.append(keep.tile([P, G1, KP], U32, name="wc%d" % ob, tag="wc%d" % ob, align_bytes=64))
+            ws.append(keep.tile([P, G1, KP], U8, name="ws%d" % ob, tag="ws%d" % ob, align_bytes=64))
+        ac = []
+        asc = []
+        for bh in range(B * NH):
+            ac.append(keep.tile([P, NIT * G2 * P], U32, name="ac%d" % bh, tag="ac%d" % bh, align_bytes=64))
+            asc.append(keep.tile([P, NIT * G2 * P], U8, name="as%d" % bh, tag="as%d" % bh, align_bytes=64))
+
+        raw_of = {}
+        grp_of = {}
+        xc = {}
+        xs = {}
+        vb = {}
+        vg = {}
+        vc = {}
+        vs = {}
+        araw_of = {}
+        agrp_of = {}
+        loaded = [0]
+
+        def load_next():
+            if loaded[0] >= len(order):
+                return
+            job = order[loaded[0]]
+            loaded[0] += 1
+            t = raw.tile([P, PACK, KP], BF16, name="raw", tag="raw")
+            if job[0] == "x":
+                c, g = job[1], job[2]
+                b, n0 = c // CPB, (c % CPB) * CH
+                src = xv[b, g * KP:(g + 1) * KP, n0:n0 + CH]
+            else:
+                g, ob = job[1], job[2]
+                src = w_v[g * KP:(g + 1) * KP, ob * KP:(ob + 1) * KP]
+            nc.sync.dma_start(out=t[:], in_=src.rearrange("(p j) n -> p j n", j=PACK))
+            raw_of[job] = t
+
+        def load_attn(r):
+            if r >= NRUN:
+                return
+            b, h, i0 = r // 8, (r // 4) % 2, 2 * (r % 4) * P
+            t = araw.tile([P, 2, D], BF16, name="araw", tag="araw")
+            nc.sync.dma_start(out=t[:], in_=attn[b, h, i0:i0 + 2 * P, :].rearrange("(a p) j -> p a j", p=P))
+            araw_of[r] = t
+
+        def copy(on_scalar, dst, src):
+            if on_scalar:
+                nc.scalar.copy(out=dst, in_=src)
+            else:
+                nc.vector.tensor_copy(out=dst, in_=src)
+
+        def interleave(job, on_scalar):
+            t = grp.tile([P, KP * PACK], BF16, name="grp", tag="grp", align_bytes=64)
+            src = raw_of.pop(job)
+            if job[0] == "x":
+                copy(on_scalar, t[:].rearrange("p (n j) -> p n j", j=PACK), src[:].rearrange("p j n -> p n j"))
+            else:
+                copy(on_scalar, t[:].rearrange("p (t m j) -> p t m j", t=PACK, j=PACK),
+                     src[:].rearrange("p j (m t) -> p t m j", t=PACK))
+            grp_of[job] = t
+            load_next()
+
+        def quantise(job):
+            t = grp_of.pop(job)
+            if job[0] == "x":
+                c, g = job[1], job[2]
+                if g == 0:
+                    xc[c] = xq.tile([P, G1, CH], U32, name="xc", tag="xc", align_bytes=64)
+                    xs[c] = xq.tile([P, G1, CH], U8, name="xs", tag="xs", align_bytes=64)
+                codes, scales = xc[c][:, g, :], xs[c][:, g, :]
+            else:
+                g, ob = job[1], job[2]
+                codes, scales = wc[ob][:, g, :], ws[ob][:, g, :]
+            nc.vector.quantize_mx(out=codes.bitcast(FP8X4), scales=scales, in_=t[:])
+
+        def s1_pass(c, ob, t, g, acc):
+            lo = t * P
+            nc.tensor.matmul_mx(
+                out=acc[:],
+                lhsT=wc[ob][:, g, lo:lo + P].bitcast(FP8X4), lhsT_scale=ws[ob][:, g, lo:lo + P],
+                rhs=xc[c][:, g, :].bitcast(FP8X4), rhs_scale=xs[c][:, g, :],
+                start=(g == 0), stop=(g == G1 - 1))
+
+        def stage1(k):
+            c, ob = s1_unit(k)
+            fresh = fresh_plan(k)
+            vb[k] = vbp.tile([P, PACK, CH], BF16, name="vb", tag="vb")
+            if fresh:
+                accs = []
+                for t in range(PACK):
+                    accs.append(psum.tile([P, CH], F32, name="bank", tag="bank"))
+                for ints, quants, g in fresh:
+                    for job, on_scalar in ints:
+                        interleave(job, on_scalar)
+                    for job in quants:
+                        quantise(job)
+                    for t in range(PACK):
+                        s1_pass(c, ob, t, g, accs[t])
+                for t in range(PACK):
+                    nc.scalar.copy(out=vb[k][:, t, :], in_=accs[t][:])
+            else:
+                for t in range(PACK):
+                    acc = psum.tile([P, CH], F32, name="bank", tag="bank")
+                    for g in range(G1):
+                        s1_pass(c, ob, t, g, acc)
+                    nc.scalar.copy(out=vb[k][:, t, :], in_=acc[:])
+
+        def v_interleave(k):
+            t = grp.tile([P, KP * PACK], BF16, name="grp", tag="grp", align_bytes=64)
+            nc.vector.tensor_copy(out=t[:].rearrange("p (n t) -> p n t", t=PACK),
+                                  in_=vb.pop(k)[:].rearrange("p t n -> p n t"))
+            vg[k] = t
+
+        def v_quantise(k):
+            c, ob = s1_unit(k)
+            h, g2 = ob // G2, ob % G2
+            if g2 == 0:
+                vc[(c, h)] = vq.tile([P, G2, CH], U32, name="vc", tag="vc", align_bytes=64)
+                vs[(c, h)] = vq.tile([P, G2, CH], U8, name="vs", tag="vs", align_bytes=64)
+            nc.vector.quantize_mx(out=vc[(c, h)][:, g2, :].bitcast(FP8X4), scales=vs[(c, h)][:, g2, :],
+                                  in_=vg.pop(k)[:])
+
+        def transposes(r):
+            src = araw_of.pop(r)
+            for a in range(2):
+                words = src[:, a, :].bitcast(F32)
+                bank = psum.tile([P, CH], F32, name="bank", tag="bank")
+                for g2 in range(G2):
+                    for u in range(2):
+                        q = g2 * 2 + u
+                        nc.tensor.transpose(bank[:, q * P:(q + 1) * P],
+                                            words[:, 256 * g2 + u:256 * (g2 + 1):2], ident[:])
+                t = agrp.tile([P, G2 * P * PACK], BF16, name="agrp", tag="agrp", align_bytes=64)
+                nc.scalar.copy(out=t[:].bitcast(F32).rearrange("p (g i u) -> p g i u", g=G2, u=2),
+                               in_=bank[:].rearrange("p (g u i) -> p g i u", g=G2, u=2))
+                agrp_of[(r, a)] = t
+            load_attn(r + 3)
+
+        def a_quantise(r):
+            bh = r // 4
+            for a in range(2):
+                lo = (2 * (r % 4) + a) * G2 * P
+                nc.vector.quantize_mx(out=ac[bh][:, lo:lo + G2 * P].bitcast(FP8X4),
+                                      scales=asc[bh][:, lo:lo + G2 * P], in_=agrp_of.pop((r, a))[:])
+
+        def stage2(j, share):
+            c, h, e = s2_unit(j)
+            b, n0 = c // CPB, (c % CPB) * CH
+            bh = b * NH + h
+            for a in range(2):
+                ot = outp.tile([P, 2, CH], F32, name="ot", tag="ot")
+                for s in range(2):
+                    it = 4 * e + 2 * a + s
+                    acc = psum.tile([P, CH], F32, name="bank", tag="bank")
+                    for g2 in range(G2):
+                        lo = (it * G2 + g2) * P
+                        nc.tensor.matmul_mx(
+                            out=acc[:],
+                            lhsT=ac[bh][:, lo:lo + P].bitcast(FP8X4), lhsT_scale=asc[bh][:, lo:lo + P],
+                            rhs=vc[(c, h)][:, g2, :].bitcast(FP8X4), rhs_scale=vs[(c, h)][:, g2, :],
+                            start=(g2 == 0), stop=(g2 == G2 - 1))
+                    copy(not (share and s == 1), ot[:, s, :], acc[:])
+                r0 = h * D + (4 * e + 2 * a) * P
+                nc.sync.dma_start(out=ov[b, r0:r0 + 2 * P, n0:n0 + CH].rearrange("(s p) n -> p s n", p=P),
+                                  in_=ot[:])
+
+        for n in range(RAW_BUFS):
+            load_next()
+        for r in range(3):
+            load_attn(r)
+
+        runs = {}
+        for r in range(NRUN):
+            runs[run_step(r)] = r
+
+        for k in range(NS1 + LAG):
+            ahead = ahead_jobs(k) if k < NS1 else []
+            if k < NS1 and fresh_plan(k):
+                stage1(k)
+            for job, on_scalar in ahead:
+                interleave(job, on_scalar)
+            if k < NS1 and not fresh_plan(k):
+                stage1(k)
+            if 0 < k <= NS1:
+                v_interleave(k - 1)
+            for job, on_scalar in ahead:
+                quantise(job)
+            if 0 < k <= NS1:
+                v_quantise(k - 1)
+            if (k - 1) in runs:
+                a_quantise(runs[k - 1])
+            if k in runs:
+                transposes(runs[k])
+            if k >= LAG:
+                stage2(k - LAG, k >= NS1)

@@ -23,10 +23,13 @@ G1 = C // KP
 G2 = D // KP
 NOB = C // KP
 NS1 = NCH * NOB
-LAG = 4
+LAG = 2
+S2_START = 8
 NIT = D // P
 RAW_BUFS = 10
-NRUN = 16
+NRUN = 8
+RUN_STEP = (5, 6, 8, 9, 16, 20, 24, 28)
+RUN_LOAD = (3, 4, 6, 7, 10, 17, 21, 25)
 
 
 def s1_unit(k):
@@ -41,12 +44,6 @@ def s2_unit(j):
     return (j // 4, (j // 2) % 2, j % 2)
 
 
-def run_step(r):
-    if r < 8:
-        return r
-    return 12 + 2 * (r - 8)
-
-
 def fresh_plan(k):
     if k == 0:
         return [([(("x", 0, g), True), (("w", g, 0), False)], [("x", 0, g), ("w", g, 0)], g) for g in range(G1)]
@@ -57,21 +54,24 @@ def fresh_plan(k):
     else:
         return []
     return [([(piece[0], False)], [piece[0]], 0),
-            ([(piece[2], True), (piece[1], False)], [piece[1]], 1),
-            ([(piece[3], False)], [piece[2]], 2),
+            ([(piece[2], False)], [piece[1]], 1),
+            ([], [piece[2]], 2),
             ([], [piece[3]], 3)]
 
 
 def ahead_jobs(k):
-    jobs = []
-    if 2 <= k < 6:
-        ob = k // 2 + 1
-        g0 = 2 * (k % 2)
-        jobs.append((("w", g0, ob), False))
-        jobs.append((("w", g0 + 1, ob), True))
-    if k >= 4 and k // 4 + 1 < NCH:
-        jobs.append((("x", k // 4 + 1, k % 4), False))
-    return jobs
+    if k == 0:
+        return [(("x", 1, 1), True, False), (("x", 1, 3), True, False)]
+    if k == 1:
+        return [(("w", 1, 1), True, False), (("w", 3, 1), True, False)]
+    g0 = 2 * (k % 2)
+    if k < 6:
+        return [(("w", g0, k // 2 + 1), False, True), (("w", g0 + 1, k // 2 + 1), True, True)]
+    if k < 8:
+        return [(("x", 2, g0), False, True), (("x", 2, g0 + 1), True, True)]
+    if k // 4 + 1 < NCH:
+        return [(("x", k // 4 + 1, k % 4), False, True)]
+    return []
 
 
 def tile_channelattention_pb_l_kernel(tc, x, w_v, attn, out):
@@ -84,18 +84,18 @@ def tile_channelattention_pb_l_kernel(tc, x, w_v, attn, out):
         for ints, quants, g in fresh_plan(k):
             for job, on_scalar in ints:
                 order.append(job)
-        for job, on_scalar in ahead_jobs(k):
+        for job, on_scalar, now in ahead_jobs(k):
             order.append(job)
 
     with ExitStack() as ctx:
         const = ctx.enter_context(tc.tile_pool(name="const", bufs=1))
         keep = ctx.enter_context(tc.tile_pool(name="keep", bufs=1))
         raw = ctx.enter_context(tc.tile_pool(name="raw", bufs=RAW_BUFS))
-        araw = ctx.enter_context(tc.tile_pool(name="araw", bufs=3))
+        araw = ctx.enter_context(tc.tile_pool(name="araw", bufs=2))
         grp = ctx.enter_context(tc.tile_pool(name="grp", bufs=4))
         agrp = ctx.enter_context(tc.tile_pool(name="agrp", bufs=4))
         xq = ctx.enter_context(tc.tile_pool(name="xq", bufs=3))
-        vbp = ctx.enter_context(tc.tile_pool(name="vbp", bufs=3))
+        vbp = ctx.enter_context(tc.tile_pool(name="vbp", bufs=2))
         vq = ctx.enter_context(tc.tile_pool(name="vq", bufs=4))
         outp = ctx.enter_context(tc.tile_pool(name="outp", bufs=3))
         psum = ctx.enter_context(tc.psum_pool(name="psum", bufs=8))
@@ -148,11 +148,9 @@ def tile_channelattention_pb_l_kernel(tc, x, w_v, attn, out):
             raw_of[job] = t
 
         def load_attn(r):
-            if r >= NRUN:
-                return
-            b, h, i0 = r // 8, (r // 4) % 2, 2 * (r % 4) * P
-            t = araw.tile([P, 2, D], BF16, name="araw", tag="araw")
-            nc.sync.dma_start(out=t[:], in_=attn[b, h, i0:i0 + 2 * P, :].rearrange("(a p) j -> p a j", p=P))
+            b, h, i0 = r // 4, (r // 2) % 2, 4 * (r % 2) * P
+            t = araw.tile([P, 4, D], BF16, name="araw", tag="araw")
+            nc.sync.dma_start(out=t[:], in_=attn[b, h, i0:i0 + 4 * P, :].rearrange("(a p) j -> p a j", p=P))
             araw_of[r] = t
 
         def copy(on_scalar, dst, src):
@@ -208,14 +206,17 @@ def tile_channelattention_pb_l_kernel(tc, x, w_v, attn, out):
                         quantise(job)
                     for t in range(PACK):
                         s1_pass(c, ob, t, g, accs[t])
-                for t in range(PACK):
-                    nc.scalar.copy(out=vb[k][:, t, :], in_=accs[t][:])
             else:
+                accs = []
                 for t in range(PACK):
-                    acc = psum.tile([P, CH], F32, name="bank", tag="bank")
+                    accs.append(psum.tile([P, CH], F32, name="bank", tag="bank"))
                     for g in range(G1):
-                        s1_pass(c, ob, t, g, acc)
-                    nc.scalar.copy(out=vb[k][:, t, :], in_=acc[:])
+                        s1_pass(c, ob, t, g, accs[t])
+            return accs
+
+        def stage1_out(k, accs):
+            for t in range(PACK):
+                nc.scalar.copy(out=vb[k][:, t, :], in_=accs[t][:])
 
         def v_interleave(k):
             t = grp.tile([P, KP * PACK], BF16, name="grp", tag="grp", align_bytes=64)
@@ -234,7 +235,7 @@ def tile_channelattention_pb_l_kernel(tc, x, w_v, attn, out):
 
         def transposes(r):
             src = araw_of.pop(r)
-            for a in range(2):
+            for a in range(4):
                 words = src[:, a, :].bitcast(F32)
                 bank = psum.tile([P, CH], F32, name="bank", tag="bank")
                 for g2 in range(G2):
@@ -246,12 +247,11 @@ def tile_channelattention_pb_l_kernel(tc, x, w_v, attn, out):
                 nc.scalar.copy(out=t[:].bitcast(F32).rearrange("p (g i u) -> p g i u", g=G2, u=2),
                                in_=bank[:].rearrange("p (g u i) -> p g i u", g=G2, u=2))
                 agrp_of[(r, a)] = t
-            load_attn(r + 3)
 
         def a_quantise(r):
-            bh = r // 4
-            for a in range(2):
-                lo = (2 * (r % 4) + a) * G2 * P
+            bh = r // 2
+            for a in range(4):
+                lo = (4 * (r % 2) + a) * G2 * P
                 nc.vector.quantize_mx(out=ac[bh][:, lo:lo + G2 * P].bitcast(FP8X4),
                                       scales=asc[bh][:, lo:lo + G2 * P], in_=agrp_of.pop((r, a))[:])
 
@@ -278,30 +278,35 @@ def tile_channelattention_pb_l_kernel(tc, x, w_v, attn, out):
 
         for n in range(RAW_BUFS):
             load_next()
-        for r in range(3):
-            load_attn(r)
-
         runs = {}
+        run_loads = {}
         for r in range(NRUN):
-            runs[run_step(r)] = r
+            runs[RUN_STEP[r]] = r
+            run_loads[RUN_LOAD[r]] = r
+        done2 = 0
 
         for k in range(NS1 + LAG):
+            if k in run_loads:
+                load_attn(run_loads[k])
             ahead = ahead_jobs(k) if k < NS1 else []
-            if k < NS1 and fresh_plan(k):
-                stage1(k)
-            for job, on_scalar in ahead:
+            if k < NS1:
+                accs = stage1(k)
+            for job, on_scalar, now in ahead:
                 interleave(job, on_scalar)
-            if k < NS1 and not fresh_plan(k):
-                stage1(k)
+            if k < NS1:
+                stage1_out(k, accs)
             if 0 < k <= NS1:
                 v_interleave(k - 1)
-            for job, on_scalar in ahead:
-                quantise(job)
+            for job, on_scalar, now in ahead:
+                if now:
+                    quantise(job)
             if 0 < k <= NS1:
                 v_quantise(k - 1)
             if (k - 1) in runs:
                 a_quantise(runs[k - 1])
             if k in runs:
                 transposes(runs[k])
-            if k >= LAG:
-                stage2(k - LAG, k >= NS1)
+            for n in range(2):
+                if k >= S2_START and done2 < NS1 and done2 <= k - LAG:
+                    stage2(done2, k >= NS1)
+                    done2 += 1

@@ -29,7 +29,7 @@ NIT = D // P
 RAW_BUFS = 10
 NRUN = 8
 RUN_STEP = (5, 6, 8, 9, 16, 20, 24, 28)
-RUN_LOAD = (3, 4, 6, 7, 10, 17, 21, 25)
+FIRST_RUN_LOAD = 3
 
 
 def s1_unit(k):
@@ -92,6 +92,7 @@ def tile_channelattention_pb_l_kernel(tc, x, w_v, attn, out):
         keep = ctx.enter_context(tc.tile_pool(name="keep", bufs=1))
         raw = ctx.enter_context(tc.tile_pool(name="raw", bufs=RAW_BUFS))
         araw = ctx.enter_context(tc.tile_pool(name="araw", bufs=2))
+        asort = ctx.enter_context(tc.tile_pool(name="asort", bufs=2))
         grp = ctx.enter_context(tc.tile_pool(name="grp", bufs=4))
         agrp = ctx.enter_context(tc.tile_pool(name="agrp", bufs=4))
         xq = ctx.enter_context(tc.tile_pool(name="xq", bufs=3))
@@ -128,6 +129,7 @@ def tile_channelattention_pb_l_kernel(tc, x, w_v, attn, out):
         vc = {}
         vs = {}
         araw_of = {}
+        asort_of = {}
         agrp_of = {}
         loaded = [0]
 
@@ -148,10 +150,21 @@ def tile_channelattention_pb_l_kernel(tc, x, w_v, attn, out):
             raw_of[job] = t
 
         def load_attn(r):
-            b, h, i0 = r // 4, (r // 2) % 2, 4 * (r % 2) * P
-            t = araw.tile([P, 4, D], BF16, name="araw", tag="araw")
-            nc.sync.dma_start(out=t[:], in_=attn[b, h, i0:i0 + 4 * P, :].rearrange("(a p) j -> p a j", p=P))
-            araw_of[r] = t
+            b, h = r // 4, (r // 2) % 2
+            for half in range(2):
+                i0 = (4 * (r % 2) + 2 * half) * P
+                t = araw.tile([P, 2, D], BF16, name="araw", tag="araw")
+                nc.sync.dma_start(out=t[:], in_=attn[b, h, i0:i0 + 2 * P, :].rearrange("(a p) j -> p a j", p=P))
+                araw_of[(r, half)] = t
+
+        def sort_attn(r):
+            for half in range(2):
+                t = asort.tile([P, 2 * D // 2], F32, name="asort", tag="asort")
+                nc.vector.tensor_copy(
+                    out=t[:].rearrange("p (q u m) -> p q u m", u=2, m=P),
+                    in_=araw_of.pop((r, half))[:].rearrange("p a j -> p (a j)").bitcast(F32).rearrange(
+                        "p (q m u) -> p q u m", u=2, m=P))
+                asort_of[(r, half)] = t
 
         def copy(on_scalar, dst, src):
             if on_scalar:
@@ -234,15 +247,13 @@ def tile_channelattention_pb_l_kernel(tc, x, w_v, attn, out):
                                   in_=vg.pop(k)[:])
 
         def transposes(r):
-            src = araw_of.pop(r)
             for a in range(4):
-                words = src[:, a, :].bitcast(F32)
+                if a % 2 == 0:
+                    src = asort_of.pop((r, a // 2))
                 bank = psum.tile([P, CH], F32, name="bank", tag="bank")
-                for g2 in range(G2):
-                    for u in range(2):
-                        q = g2 * 2 + u
-                        nc.tensor.transpose(bank[:, q * P:(q + 1) * P],
-                                            words[:, 256 * g2 + u:256 * (g2 + 1):2], ident[:])
+                for q in range(2 * G2):
+                    lo = ((a % 2) * 2 * G2 + q) * P
+                    nc.tensor.transpose(bank[:, q * P:(q + 1) * P], src[:, lo:lo + P], ident[:])
                 t = agrp.tile([P, G2 * P * PACK], BF16, name="agrp", tag="agrp", align_bytes=64)
                 nc.scalar.copy(out=t[:].bitcast(F32).rearrange("p (g i u) -> p g i u", g=G2, u=2),
                                in_=bank[:].rearrange("p (g u i) -> p g i u", g=G2, u=2))
@@ -279,15 +290,15 @@ def tile_channelattention_pb_l_kernel(tc, x, w_v, attn, out):
         for n in range(RAW_BUFS):
             load_next()
         runs = {}
-        run_loads = {}
         for r in range(NRUN):
             runs[RUN_STEP[r]] = r
-            run_loads[RUN_LOAD[r]] = r
         done2 = 0
 
         for k in range(NS1 + LAG):
-            if k in run_loads:
-                load_attn(run_loads[k])
+            if k == FIRST_RUN_LOAD:
+                load_attn(0)
+            if k in runs and runs[k] + 1 < NRUN:
+                load_attn(runs[k] + 1)
             ahead = ahead_jobs(k) if k < NS1 else []
             if k < NS1:
                 accs = stage1(k)
@@ -306,6 +317,8 @@ def tile_channelattention_pb_l_kernel(tc, x, w_v, attn, out):
                 a_quantise(runs[k - 1])
             if k in runs:
                 transposes(runs[k])
+            if (k + 1) in runs:
+                sort_attn(runs[k + 1])
             for n in range(2):
                 if k >= S2_START and done2 < NS1 and done2 <= k - LAG:
                     stage2(done2, k >= NS1)

@@ -26,7 +26,7 @@ NS1 = NCH * NOB
 LAG = 2
 S2_START = 8
 NIT = D // P
-RAW_BUFS = 10
+RAW_BUFS = 5
 NRUN = 8
 RUN_STEP = (5, 6, 8, 9, 16, 20, 24, 28)
 FIRST_RUN_LOAD = 3
@@ -45,25 +45,21 @@ def s2_unit(j):
 
 
 def fresh_plan(k):
-    if k == 0:
-        return [([(("x", 0, g), True), (("w", g, 0), False)], [("x", 0, g), ("w", g, 0)], g) for g in range(G1)]
-    if k == 1:
-        piece = [("x", 1, g) for g in range(G1)]
-    elif k == 2:
-        piece = [("w", g, 1) for g in range(G1)]
-    else:
+    if k != 0:
         return []
-    return [([(piece[0], False)], [piece[0]], 0),
-            ([(piece[2], False)], [piece[1]], 1),
-            ([], [piece[2]], 2),
-            ([], [piece[3]], 3)]
+    return [([(("x", 0, g), True), (("x", 1, g), True), (("w", g, 0), False), (("w", g, 1), False)],
+             [("x", 0, g), ("w", g, 0), ("w", g, 1), ("x", 1, g)], g) for g in range(G1)]
+
+
+def raw_key(job):
+    if job[0] == "x":
+        return (("X", job[1] // 2, job[2]), job[1] % 2)
+    return (("W", job[1], job[2] // 2), job[2] % 2)
 
 
 def ahead_jobs(k):
-    if k == 0:
-        return [(("x", 1, 1), True, False), (("x", 1, 3), True, False)]
-    if k == 1:
-        return [(("w", 1, 1), True, False), (("w", 3, 1), True, False)]
+    if k < 2:
+        return []
     g0 = 2 * (k % 2)
     if k < 6:
         return [(("w", g0, k // 2 + 1), False, True), (("w", g0 + 1, k // 2 + 1), True, True)]
@@ -83,9 +79,11 @@ def tile_channelattention_pb_l_kernel(tc, x, w_v, attn, out):
     for k in range(NS1):
         for ints, quants, g in fresh_plan(k):
             for job, on_scalar in ints:
-                order.append(job)
+                if raw_key(job)[0] not in order:
+                    order.append(raw_key(job)[0])
         for job, on_scalar, now in ahead_jobs(k):
-            order.append(job)
+            if raw_key(job)[0] not in order:
+                order.append(raw_key(job)[0])
 
     with ExitStack() as ctx:
         const = ctx.enter_context(tc.tile_pool(name="const", bufs=1))
@@ -98,7 +96,7 @@ def tile_channelattention_pb_l_kernel(tc, x, w_v, attn, out):
         xq = ctx.enter_context(tc.tile_pool(name="xq", bufs=3))
         vbp = ctx.enter_context(tc.tile_pool(name="vbp", bufs=2))
         vq = ctx.enter_context(tc.tile_pool(name="vq", bufs=4))
-        outp = ctx.enter_context(tc.tile_pool(name="outp", bufs=3))
+        outp = ctx.enter_context(tc.tile_pool(name="outp", bufs=4))
         psum = ctx.enter_context(tc.psum_pool(name="psum", bufs=8))
         ctx.enter_context(tc.manual_schedule())
 
@@ -121,6 +119,8 @@ def tile_channelattention_pb_l_kernel(tc, x, w_v, attn, out):
             asc.append(keep.tile([P, NIT * G2 * P], U8, name="as%d" % bh, tag="as%d" % bh, align_bytes=64))
 
         raw_of = {}
+        uses = {}
+        pair = []
         grp_of = {}
         xc = {}
         xs = {}
@@ -136,18 +136,19 @@ def tile_channelattention_pb_l_kernel(tc, x, w_v, attn, out):
         def load_next():
             if loaded[0] >= len(order):
                 return
-            job = order[loaded[0]]
+            key = order[loaded[0]]
             loaded[0] += 1
-            t = raw.tile([P, PACK, KP], BF16, name="raw", tag="raw")
-            if job[0] == "x":
-                c, g = job[1], job[2]
-                b, n0 = c // CPB, (c % CPB) * CH
-                src = xv[b, g * KP:(g + 1) * KP, n0:n0 + CH]
+            t = raw.tile([P, PACK, 2 * KP], BF16, name="raw", tag="raw")
+            if key[0] == "X":
+                sc, g = key[1], key[2]
+                b, n0 = 2 * sc // CPB, (2 * sc % CPB) * CH
+                src = xv[b, g * KP:(g + 1) * KP, n0:n0 + 2 * CH]
             else:
-                g, ob = job[1], job[2]
-                src = w_v[g * KP:(g + 1) * KP, ob * KP:(ob + 1) * KP]
+                g, hw = key[1], key[2]
+                src = w_v[g * KP:(g + 1) * KP, hw * 2 * KP:(hw + 1) * 2 * KP]
             nc.sync.dma_start(out=t[:], in_=src.rearrange("(p j) n -> p j n", j=PACK))
-            raw_of[job] = t
+            raw_of[key] = t
+            uses[key] = 2
 
         def load_attn(r):
             b, h = r // 4, (r // 2) % 2
@@ -174,14 +175,18 @@ def tile_channelattention_pb_l_kernel(tc, x, w_v, attn, out):
 
         def interleave(job, on_scalar):
             t = grp.tile([P, KP * PACK], BF16, name="grp", tag="grp", align_bytes=64)
-            src = raw_of.pop(job)
+            key, half = raw_key(job)
+            src = raw_of[key][:, :, half * KP:(half + 1) * KP]
             if job[0] == "x":
-                copy(on_scalar, t[:].rearrange("p (n j) -> p n j", j=PACK), src[:].rearrange("p j n -> p n j"))
+                copy(on_scalar, t[:].rearrange("p (n j) -> p n j", j=PACK), src.rearrange("p j n -> p n j"))
             else:
                 copy(on_scalar, t[:].rearrange("p (t m j) -> p t m j", t=PACK, j=PACK),
-                     src[:].rearrange("p j (m t) -> p t m j", t=PACK))
+                     src.rearrange("p j (m t) -> p t m j", t=PACK))
             grp_of[job] = t
-            load_next()
+            uses[key] -= 1
+            if uses[key] == 0:
+                raw_of.pop(key)
+                load_next()
 
         def quantise(job):
             t = grp_of.pop(job)
@@ -212,13 +217,19 @@ def tile_channelattention_pb_l_kernel(tc, x, w_v, attn, out):
                 accs = []
                 for t in range(PACK):
                     accs.append(psum.tile([P, CH], F32, name="bank", tag="bank"))
+                for t in range(PACK):
+                    pair.append(psum.tile([P, CH], F32, name="bank", tag="bank"))
                 for ints, quants, g in fresh:
                     for job, on_scalar in ints:
                         interleave(job, on_scalar)
                     for job in quants:
                         quantise(job)
                     for t in range(PACK):
-                        s1_pass(c, ob, t, g, accs[t])
+                        s1_pass(0, 0, t, g, accs[t])
+                    for t in range(PACK):
+                        s1_pass(1, 0, t, g, pair[t])
+            elif k == 1:
+                accs = pair
             else:
                 accs = []
                 for t in range(PACK):

from contextlib import ExitStack

import concourse.mybir as mybir
from concourse.masks import make_identity

B, C, NTOK, NH = 2, 2048, 4096, 2
D = C // NH
FLOPS = 2 * B * NTOK * C * C + 2 * B * NH * D * D * NTOK

F32 = mybir.dt.float32
BF16 = mybir.dt.bfloat16
U32 = mybir.dt.uint32
U8 = mybir.dt.uint8
FP8X4 = mybir.dt.float8_e4m3fn_x4

P = 128
PACK = 4
KP = P * PACK
CH = 512
NCH = B * NTOK // CH
CPB = NTOK // CH
G1 = C // KP
G2 = D // KP
NOB = C // KP
NS1 = NCH * NOB
LAG = 2
S2_START = 8
NIT = D // P
RAW_BUFS = 5
NRUN = 8
RUN_STEP = (5, 6, 8, 9, 16, 20, 24, 28)
FIRST_RUN_LOAD = 3


def s1_unit(k):
    if k < 2 * NOB:
        return (k % 2, k // 2)
    return (k // NOB, k % NOB)


def s2_unit(j):
    if j < 2 * NOB:
        return ((j // 2) % 2, j // 4, j % 2)
    return (j // 4, (j // 2) % 2, j % 2)


def fresh_plan(k):
    if k != 0:
        return []
    return [([(("x", 0, g), True), (("x", 1, g), True), (("w", g, 0), False), (("w", g, 1), False)],
             [("x", 0, g), ("w", g, 0), ("w", g, 1), ("x", 1, g)], g) for g in range(G1)]


def raw_key(job):
    if job[0] == "x":
        return (("X", job[1] // 2, job[2]), job[1] % 2)
    return (("W", job[1], job[2] // 2), job[2] % 2)


def ahead_jobs(k):
    if k < 2:
        return []
    g0 = 2 * (k % 2)
    if k < 6:
        return [(("w", g0, k // 2 + 1), False, True), (("w", g0 + 1, k // 2 + 1), True, True)]
    if k < 8:
        return [(("x", 2, g0), False, True), (("x", 2, g0 + 1), True, True)]
    if k // 4 + 1 < NCH:
        return [(("x", k // 4 + 1, k % 4), False, True)]
    return []


def tile_channelattention_pb_l_kernel(tc, x, w_v, attn, out):
    nc = tc.nc
    xv = x.rearrange("b c w h z -> b c (w h z)")
    ov = out.rearrange("b c w h z -> b c (w h z)")

    order = []
    for k in range(NS1):
        for ints, quants, g in fresh_plan(k):
            for job, on_scalar in ints:
                if raw_key(job)[0] not in order:
                    order.append(raw_key(job)[0])
        for job, on_scalar, now in ahead_jobs(k):
            if raw_key(job)[0] not in order:
                order.append(raw_key(job)[0])

    with ExitStack() as ctx:
        const = ctx.enter_context(tc.tile_pool(name="const", bufs=1))
        keep = ctx.enter_context(tc.tile_pool(name="keep", bufs=1))
        raw = ctx.enter_context(tc.tile_pool(name="raw", bufs=RAW_BUFS))
        araw = ctx.enter_context(tc.tile_pool(name="araw", bufs=2))
        asort = ctx.enter_context(tc.tile_pool(name="asort", bufs=2))
        grp = ctx.enter_context(tc.tile_pool(name="grp", bufs=4))
        agrp = ctx.enter_context(tc.tile_pool(name="agrp", bufs=4))
        xq = ctx.enter_context(tc.tile_pool(name="xq", bufs=3))
        vbp = ctx.enter_context(tc.tile_pool(name="vbp", bufs=2))
        vq = ctx.enter_context(tc.tile_pool(name="vq", bufs=4))
        outp = ctx.enter_context(tc.tile_pool(name="outp", bufs=4))
        psum = ctx.enter_context(tc.psum_pool(name="psum", bufs=8))
        ctx.enter_context(tc.manual_schedule())

        warm_in = const.tile([P, 8], F32, name="warm_in", tag="warm_in")
        warm_out = const.tile([P, 8], F32, name="warm_out", tag="warm_out")
        nc.vector.memset(warm_in[:], 0.0)
        nc.scalar.copy(out=warm_out[:], in_=warm_in[:])
        ident = const.tile([P, P], F32, name="ident", tag="ident")
        make_identity(nc, ident[:])

        wc = []
        ws = []
        for ob in range(NOB):
            wc.append(keep.tile([P, G1, KP], U32, name="wc%d" % ob, tag="wc%d" % ob, align_bytes=64))
            ws.append(keep.tile([P, G1, KP], U8, name="ws%d" % ob, tag="ws%d" % ob, align_bytes=64))
        ac = []
        asc = []
        for bh in range(B * NH):
            ac.append(keep.tile([P, NIT * G2 * P], U32, name="ac%d" % bh, tag="ac%d" % bh, align_bytes=64))
            asc.append(keep.tile([P, NIT * G2 * P], U8, name="as%d" % bh, tag="as%d" % bh, align_bytes=64))

        raw_of = {}
        uses = {}
        pair = []
        grp_of = {}
        xc = {}
        xs = {}
        vb = {}
        vg = {}
        vc = {}
        vs = {}
        araw_of = {}
        asort_of = {}
        agrp_of = {}
        loaded = [0]

        def load_next():
            if loaded[0] >= len(order):
                return
            key = order[loaded[0]]
            loaded[0] += 1
            t = raw.tile([P, PACK, 2 * KP], BF16, name="raw", tag="raw")
            if key[0] == "X":
                sc, g = key[1], key[2]
                b, n0 = 2 * sc // CPB, (2 * sc % CPB) * CH
                src = xv[b, g * KP:(g + 1) * KP, n0:n0 + 2 * CH]
            else:
                g, hw = key[1], key[2]
                src = w_v[g * KP:(g + 1) * KP, hw * 2 * KP:(hw + 1) * 2 * KP]
            nc.sync.dma_start(out=t[:], in_=src.rearrange("(p j) n -> p j n", j=PACK))
            raw_of[key] = t
            uses[key] = 2

        def load_attn(r):
            b, h = r // 4, (r // 2) % 2
            for half in range(2):
                i0 = (4 * (r % 2) + 2 * half) * P
                t = araw.tile([P, 2, D], BF16, name="araw", tag="araw")
                nc.sync.dma_start(out=t[:], in_=attn[b, h, i0:i0 + 2 * P, :].rearrange("(a p) j -> p a j", p=P))
                araw_of[(r, half)] = t

        def sort_attn(r):
            for half in range(2):
                t = asort.tile([P, 2 * D // 2], F32, name="asort", tag="asort")
                nc.vector.tensor_copy(
                    out=t[:].rearrange("p (q u m) -> p q u m", u=2, m=P),
                    in_=araw_of.pop((r, half))[:].rearrange("p a j -> p (a j)").bitcast(F32).rearrange(
                        "p (q m u) -> p q u m", u=2, m=P))
                asort_of[(r, half)] = t

        def copy(on_scalar, dst, src):
            if on_scalar:
                nc.scalar.copy(out=dst, in_=src)
            else:
                nc.vector.tensor_copy(out=dst, in_=src)

        def interleave(job, on_scalar):
            t = grp.tile([P, KP * PACK], BF16, name="grp", tag="grp", align_bytes=64)
            key, half = raw_key(job)
            src = raw_of[key][:, :, half * KP:(half + 1) * KP]
            if job[0] == "x":
                copy(on_scalar, t[:].rearrange("p (n j) -> p n j", j=PACK), src.rearrange("p j n -> p n j"))
            else:
                copy(on_scalar, t[:].rearrange("p (t m j) -> p t m j", t=PACK, j=PACK),
                     src.rearrange("p j (m t) -> p t m j", t=PACK))
            grp_of[job] = t
            uses[key] -= 1
            if uses[key] == 0:
                raw_of.pop(key)
                load_next()

        def quantise(job):
            t = grp_of.pop(job)
            if job[0] == "x":
                c, g = job[1], job[2]
                if g == 0:
                    xc[c] = xq.tile([P, G1, CH], U32, name="xc", tag="xc", align_bytes=64)
                    xs[c] = xq.tile([P, G1, CH], U8, name="xs", tag="xs", align_bytes=64)
                codes, scales = xc[c][:, g, :], xs[c][:, g, :]
            else:
                g, ob = job[1], job[2]
                codes, scales = wc[ob][:, g, :], ws[ob][:, g, :]
            nc.vector.quantize_mx(out=codes.bitcast(FP8X4), scales=scales, in_=t[:])

        def s1_pass(c, ob, t, g, acc):
            lo = t * P
            nc.tensor.matmul_mx(
                out=acc[:],
                lhsT=wc[ob][:, g, lo:lo + P].bitcast(FP8X4), lhsT_scale=ws[ob][:, g, lo:lo + P],
                rhs=xc[c][:, g, :].bitcast(FP8X4), rhs_scale=xs[c][:, g, :],
                start=(g == 0), stop=(g == G1 - 1))

        def stage1(k):
            c, ob = s1_unit(k)
            fresh = fresh_plan(k)
            vb[k] = vbp.tile([P, PACK, CH], BF16, name="vb", tag="vb")
            if fresh:
                accs = []
                for t in range(PACK):
                    accs.append(psum.tile([P, CH], F32, name="bank", tag="bank"))
                for t in range(PACK):
                    pair.append(psum.tile([P, CH], F32, name="bank", tag="bank"))
                for ints, quants, g in fresh:
                    for job, on_scalar in ints:
                        interleave(job, on_scalar)
                    for job in quants:
                        quantise(job)
                    for t in range(PACK):
                        s1_pass(0, 0, t, g, accs[t])
                    for t in range(PACK):
                        s1_pass(1, 0, t, g, pair[t])
            elif k == 1:
                accs = pair
            else:
                accs = []
                for t in range(PACK):
                    accs.append(psum.tile([P, CH], F32, name="bank", tag="bank"))
                    for g in range(G1):
                        s1_pass(c, ob, t, g, accs[t])
            return accs

        def stage1_out(k, accs):
            for t in range(PACK):
                nc.scalar.copy(out=vb[k][:, t, :], in_=accs[t][:])

        def v_interleave(k):
            t = grp.tile([P, KP * PACK], BF16, name="grp", tag="grp", align_bytes=64)
            nc.vector.tensor_copy(out=t[:].rearrange("p (n t) -> p n t", t=PACK),
                                  in_=vb.pop(k)[:].rearrange("p t n -> p n t"))
            vg[k] = t

        def v_quantise(k):
            c, ob = s1_unit(k)
            h, g2 = ob // G2, ob % G2
            if g2 == 0:
                vc[(c, h)] = vq.tile([P, G2, CH], U32, name="vc", tag="vc", align_bytes=64)
                vs[(c, h)] = vq.tile([P, G2, CH], U8, name="vs", tag="vs", align_bytes=64)
            nc.vector.quantize_mx(out=vc[(c, h)][:, g2, :].bitcast(FP8X4), scales=vs[(c, h)][:, g2, :],
                                  in_=vg.pop(k)[:])

        def transposes(r):
            for a in range(4):
                if a % 2 == 0:
                    src = asort_of.pop((r, a // 2))
                bank = psum.tile([P, CH], F32, name="bank", tag="bank")
                for q in range(2 * G2):
                    lo = ((a % 2) * 2 * G2 + q) * P
                    nc.tensor.transpose(bank[:, q * P:(q + 1) * P], src[:, lo:lo + P], ident[:])
                t = agrp.tile([P, G2 * P * PACK], BF16, name="agrp", tag="agrp", align_bytes=64)
                nc.scalar.copy(out=t[:].bitcast(F32).rearrange("p (g i u) -> p g i u", g=G2, u=2),
                               in_=bank[:].rearrange("p (g u i) -> p g i u", g=G2, u=2))
                agrp_of[(r, a)] = t

        def a_quantise(r):
            bh = r // 2
            for a in range(4):
                lo = (4 * (r % 2) + a) * G2 * P
                nc.vector.quantize_mx(out=ac[bh][:, lo:lo + G2 * P].bitcast(FP8X4),
                                      scales=asc[bh][:, lo:lo + G2 * P], in_=agrp_of.pop((r, a))[:])

        def stage2(j, share):
            c, h, e = s2_unit(j)
            b, n0 = c // CPB, (c % CPB) * CH
            bh = b * NH + h
            for a in range(2):
                ot = outp.tile([P, 2, CH], F32, name="ot", tag="ot")
                for s in range(2):
                    it = 4 * e + 2 * a + s
                    acc = psum.tile([P, CH], F32, name="bank", tag="bank")
                    for g2 in range(G2):
                        lo = (it * G2 + g2) * P
                        nc.tensor.matmul_mx(
                            out=acc[:],
                            lhsT=ac[bh][:, lo:lo + P].bitcast(FP8X4), lhsT_scale=asc[bh][:, lo:lo + P],
                            rhs=vc[(c, h)][:, g2, :].bitcast(FP8X4), rhs_scale=vs[(c, h)][:, g2, :],
                            start=(g2 == 0), stop=(g2 == G2 - 1))
                    copy(not (share and s == 1), ot[:, s, :], acc[:])
                r0 = h * D + (4 * e + 2 * a) * P
                nc.sync.dma_start(out=ov[b, r0:r0 + 2 * P, n0:n0 + CH].rearrange("(s p) n -> p s n", p=P),
                                  in_=ot[:])

        for n in range(RAW_BUFS):
            load_next()
        runs = {}
        for r in range(NRUN):
            runs[RUN_STEP[r]] = r
        done2 = 0

        for k in range(NS1 + LAG):
            if k == FIRST_RUN_LOAD:
                load_attn(0)
            if k in runs and runs[k] + 1 < NRUN:
                load_attn(runs[k] + 1)
            ahead = ahead_jobs(k) if k < NS1 else []
            if k < NS1:
                accs = stage1(k)
            for job, on_scalar, now in ahead:
                interleave(job, on_scalar)
            if k < NS1:
                stage1_out(k, accs)
            if 0 < k <= NS1:
                v_interleave(k - 1)
            for job, on_scalar, now in ahead:
                if now:
                    quantise(job)
            if 0 < k <= NS1:
                v_quantise(k - 1)
            if (k - 1) in runs:
                a_quantise(runs[k - 1])
            if k in runs:
                transposes(runs[k])
            if (k + 1) in runs:
                sort_attn(runs[k + 1])
            for n in range(2):
                if k >= S2_START and done2 < NS1 and done2 <= k - LAG:
                    stage2(done2, k >= NS1)
                    done2 += 1
